import numpy as np
import ml_dtypes

BF16 = ml_dtypes.bfloat16


def bf(x):
    return np.asarray(x, np.float32).astype(BF16)


def f32(x):
    return np.asarray(x, np.float32)


def f64(x):
    return np.asarray(x).astype(np.float64)


def striped(idx):
    return np.tile(idx.reshape(-1, 16).T, (8, 1))


D, DK, H, E, M, S, N = 128, 128, 2, 3, 256, 4096, 512
EV_A = ((1.0, 0.3, -0.2), (0.8, -0.3, 0.25))
EV_B = ((0.2, -0.3, 0.1), (-0.15, 0.25, 0.3))


def setup_inputs():
    return {"table": bf(np.random.standard_normal((D, S))), "wq": bf(np.random.standard_normal((D, M)) / np.sqrt(D)), "wk": bf(np.random.standard_normal((D, M)) / np.sqrt(D)), "offs": striped(np.random.permutation(S)[:N])}


def reference(table, wq, wk, offs):
    idx = offs[:16].T.reshape(-1)
    z = f64(table)
    q = f64(wq).T @ z[:, idx]
    key = f64(wk).T @ z
    u = np.zeros((S, N))
    for h in range(H):
        r = slice(h * DK, (h + 1) * DK)
        sc = key[r].T @ q[r] / np.sqrt(DK)
        ex = [np.exp(EV_A[h][e] * sc + EV_B[h][e]) for e in range(E)]
        u = u + sc * ex[0] / sum(ex)
    return u / H

@@ -1,0 +1,125 @@
+import math
+
+import concourse.mybir as mybir
+
+F32 = mybir.dt.float32
+BF16 = mybir.dt.bfloat16
+U16 = mybir.dt.uint16
+FUNC = mybir.ActivationFunctionType
+ALU = mybir.AluOpType
+
+P = 128
+HEADS = 2
+GENES = 4096
+PICKED = 512
+BLOCKS = GENES // P
+LOAD_COLS = 1024
+PROJ_COLS = 512
+BLOCKS_PER_PROJ = PROJ_COLS // P
+
+EV_A = ((1.0, 0.3, -0.2), (0.8, -0.3, 0.25))
+EV_B = ((0.2, -0.3, 0.1), (-0.15, 0.25, 0.3))
+INV_SQRT_DK = 1.0 / math.sqrt(P)
+LN_TOP = 2.0**63
+
+FLOPS = 2 * P * HEADS * P * (PICKED + GENES) + 2 * HEADS * P * GENES * PICKED
+
+
+def flat_and_steep(h):
+    terms = [(EV_A[h][e] - EV_A[h][0], EV_B[h][e] - EV_B[h][0]) for e in (1, 2)]
+    flat, steep = sorted(terms, reverse=True)
+    assert steep[0] < flat[0] and steep[0] < 0.0
+    return flat, steep
+
+
+def tile_multiheadefralayer_nomp_kernel(tc, table, wq, wk, offs, out):
+    nc = tc.nc
+    terms = [flat_and_steep(h) for h in range(HEADS)]
+
+    with tc.tile_pool(name="held", bufs=1) as held:
+        offsets = held.tile([P, PICKED // 16], U16, name="offsets")
+        nc.sync.dma_start(offsets[:], offs)
+        wq_sb = held.tile([P, HEADS * P], BF16, name="wq_sb")
+        nc.scalar.dma_start(wq_sb[:], wq)
+        wk_sb = held.tile([P, HEADS * P], BF16, name="wk_sb")
+        nc.scalar.dma_start(wk_sb[:], wk)
+        table_sb = held.tile([P, GENES], BF16, name="table_sb")
+        for c in range(GENES // LOAD_COLS):
+            queue = nc.sync if c % 2 == 0 else nc.scalar
+            cols = slice(c * LOAD_COLS, (c + 1) * LOAD_COLS)
+            queue.dma_start(table_sb[:, cols], table[:, cols])
+
+        consts = held.tile([P, 1 + 2 * HEADS], F32, name="consts")
+        one = consts[:, 0:1]
+        nc.vector.memset(one, 1.0)
+        exp_bias = [consts[:, 1 + h : 2 + h] for h in range(HEADS)]
+        sig_bias = [consts[:, 1 + HEADS + h : 2 + HEADS + h] for h in range(HEADS)]
+        for h, (flat, steep) in enumerate(terms):
+            nc.vector.memset(exp_bias[h], steep[1] - flat[1])
+            nc.vector.memset(sig_bias[h], -flat[1])
+
+        q_bf = [held.tile([P, PICKED], BF16, name=f"q_bf{h}") for h in range(HEADS)]
+        key_bf = [held.tile([P, GENES], BF16, name=f"key_bf{h}") for h in range(HEADS)]
+        kept = [held.tile([P, BLOCKS * PICKED], F32, name=f"kept{h}") for h in range(HEADS)]
+
+        def raw_scores(psum, h, b):
+            x = psum.tile([P, PICKED], F32, name="x")
+            nc.tensor.matmul(x[:], key_bf[h][:, b * P : (b + 1) * P], q_bf[h][:], start=True, stop=True)
+            return x
+
+        with (
+            tc.psum_pool(name="proj_psum", bufs=2) as proj_psum,
+            tc.psum_pool(name="exp_psum", bufs=6) as exp_psum,
+            tc.tile_pool(name="exp_work", bufs=4) as exp_work,
+        ):
+            for h in range(HEADS):
+                q_ps = proj_psum.tile([P, PICKED], F32, tag="proj")
+                nc.tensor.matmul(
+                    q_ps[:], wq_sb[:, h * P : (h + 1) * P], table_sb[:].indirect(offsets[:]), start=True, stop=True
+                )
+                nc.vector.tensor_copy(q_bf[h][:], q_ps[:])
+            for c in range(GENES // PROJ_COLS):
+                cols = slice(c * PROJ_COLS, (c + 1) * PROJ_COLS)
+                for h in range(HEADS):
+                    key_ps = proj_psum.tile([P, PROJ_COLS], F32, tag="proj")
+                    nc.tensor.matmul(key_ps[:], wk_sb[:, h * P : (h + 1) * P], table_sb[:, cols], start=True, stop=True)
+                    nc.vector.tensor_copy(key_bf[h][:, cols], key_ps[:])
+                for b in range(c * BLOCKS_PER_PROJ, (c + 1) * BLOCKS_PER_PROJ):
+                    for h, (flat, steep) in enumerate(terms):
+                        x = raw_scores(exp_psum, h, b)
+                        r = exp_work.tile([P, PICKED], F32, name="r")
+                        nc.scalar.activation(
+                            r[:], x[:], FUNC.Exp, bias=exp_bias[h], scale=(steep[0] - flat[0]) * INV_SQRT_DK
+                        )
+                        nc.vector.tensor_scalar_min(kept[h][:, b * PICKED : (b + 1) * PICKED], r[:], LN_TOP)
+
+        with (
+            tc.psum_pool(name="log_psum", bufs=8) as log_psum,
+            tc.tile_pool(name="log_work", bufs=4) as log_work,
+        ):
+            for b in range(BLOCKS):
+                for h, (flat, steep) in enumerate(terms):
+                    block = kept[h][:, b * PICKED : (b + 1) * PICKED]
+                    log1p = log_work.tile([P, PICKED], F32, name="log1p")
+                    nc.scalar.activation(log1p[:], block, FUNC.Ln, bias=one, scale=1.0)
+                    x = raw_scores(log_psum, h, b)
+                    nc.vector.scalar_tensor_tensor(block, x[:], flat[0] * INV_SQRT_DK, log1p[:], ALU.mult, ALU.add)
+
+        with (
+            tc.psum_pool(name="out_psum", bufs=8) as out_psum,
+            tc.tile_pool(name="out_work", bufs=4) as out_work,
+        ):
+            for b in range(BLOCKS):
+                weighted = []
+                for h in range(HEADS):
+                    a = out_work.tile([P, PICKED], F32, name="a")
+                    nc.scalar.activation(
+                        a[:], kept[h][:, b * PICKED : (b + 1) * PICKED], FUNC.Sigmoid, bias=sig_bias[h], scale=-1.0
+                    )
+                    x = raw_scores(out_psum, h, b)
+                    half_as = out_work.tile([P, PICKED], F32, name=f"half_as{h}")
+                    nc.vector.scalar_tensor_tensor(half_as[:], x[:], 0.5 * INV_SQRT_DK, a[:], ALU.mult, ALU.mult)
+                    weighted.append(half_as)
+                total = out_work.tile([P, PICKED], F32, name="total")
+                nc.gpsimd.tensor_tensor(total[:], weighted[0][:], weighted[1][:], ALU.add)
+                nc.sync.dma_start(out[b * P : (b + 1) * P, :], total[:])

@@ -16,6 +16,8 @@ BLOCKS = GENES // P
 LOAD_COLS = 1024
 PROJ_COLS = 512
 BLOCKS_PER_PROJ = PROJ_COLS // P
+PAIR = 2
+PAIRS = BLOCKS // PAIR
 
 EV_A = ((1.0, 0.3, -0.2), (0.8, -0.3, 0.25))
 EV_B = ((0.2, -0.3, 0.1), (-0.15, 0.25, 0.3))
@@ -45,9 +47,8 @@ def tile_multiheadefralayer_nomp_kernel(tc, table, wq, wk, offs, out):
         nc.scalar.dma_start(wk_sb[:], wk)
         table_sb = held.tile([P, GENES], BF16, name="table_sb")
         for c in range(GENES // LOAD_COLS):
-            queue = nc.sync if c % 2 == 0 else nc.scalar
             cols = slice(c * LOAD_COLS, (c + 1) * LOAD_COLS)
-            queue.dma_start(table_sb[:, cols], table[:, cols])
+            nc.sync.dma_start(table_sb[:, cols], table[:, cols])
 
         consts = held.tile([P, 1 + 2 * HEADS], F32, name="consts")
         one = consts[:, 0:1]
@@ -97,29 +98,50 @@ def tile_multiheadefralayer_nomp_kernel(tc, table, wq, wk, offs, out):
             tc.psum_pool(name="log_psum", bufs=8) as log_psum,
             tc.tile_pool(name="log_work", bufs=4) as log_work,
         ):
-            for b in range(BLOCKS):
+            for pair in range(PAIRS):
                 for h, (flat, steep) in enumerate(terms):
-                    block = kept[h][:, b * PICKED : (b + 1) * PICKED]
-                    log1p = log_work.tile([P, PICKED], F32, name="log1p")
-                    nc.scalar.activation(log1p[:], block, FUNC.Ln, bias=one, scale=1.0)
-                    x = raw_scores(log_psum, h, b)
-                    nc.vector.scalar_tensor_tensor(block, x[:], flat[0] * INV_SQRT_DK, log1p[:], ALU.mult, ALU.add)
+                    log1p = log_work.tile([P, PAIR * PICKED], F32, name="log1p")
+                    pair_cols = slice(pair * PAIR * PICKED, (pair + 1) * PAIR * PICKED)
+                    nc.scalar.activation(log1p[:], kept[h][:, pair_cols], FUNC.Ln, bias=one, scale=1.0)
+                    for k in range(PAIR):
+                        b = pair * PAIR + k
+                        x = raw_scores(log_psum, h, b)
+                        nc.vector.scalar_tensor_tensor(
+                            kept[h][:, b * PICKED : (b + 1) * PICKED],
+                            x[:],
+                            flat[0] * INV_SQRT_DK,
+                            log1p[:, k * PICKED : (k + 1) * PICKED],
+                            ALU.mult,
+                            ALU.add,
+                        )
 
         with (
             tc.psum_pool(name="out_psum", bufs=8) as out_psum,
-            tc.tile_pool(name="out_work", bufs=4) as out_work,
+            tc.tile_pool(name="out_work", bufs=3) as out_work,
         ):
-            for b in range(BLOCKS):
+            for pair in range(PAIRS):
                 weighted = []
                 for h in range(HEADS):
-                    a = out_work.tile([P, PICKED], F32, name="a")
-                    nc.scalar.activation(
-                        a[:], kept[h][:, b * PICKED : (b + 1) * PICKED], FUNC.Sigmoid, bias=sig_bias[h], scale=-1.0
-                    )
-                    x = raw_scores(out_psum, h, b)
-                    half_as = out_work.tile([P, PICKED], F32, name=f"half_as{h}")
-                    nc.vector.scalar_tensor_tensor(half_as[:], x[:], 0.5 * INV_SQRT_DK, a[:], ALU.mult, ALU.mult)
+                    a = out_work.tile([P, PAIR * PICKED], F32, name="a")
+                    pair_cols = slice(pair * PAIR * PICKED, (pair + 1) * PAIR * PICKED)
+                    nc.scalar.activation(a[:], kept[h][:, pair_cols], FUNC.Sigmoid, bias=sig_bias[h], scale=-1.0)
+                    half_as = out_work.tile([P, PAIR * PICKED], F32, name=f"half_as{h}")
+                    for k in range(PAIR):
+                        cols = slice(k * PICKED, (k + 1) * PICKED)
+                        x = raw_scores(out_psum, h, pair * PAIR + k)
+                        nc.vector.scalar_tensor_tensor(
+                            half_as[:, cols], x[:], 0.5 * INV_SQRT_DK, a[:, cols], ALU.mult, ALU.mult
+                        )
                     weighted.append(half_as)
-                total = out_work.tile([P, PICKED], F32, name="total")
-                nc.gpsimd.tensor_tensor(total[:], weighted[0][:], weighted[1][:], ALU.add)
-                nc.sync.dma_start(out[b * P : (b + 1) * P, :], total[:])
+                total = out_work.tile([P, PAIR * PICKED], F32, name="total")
+                rows = out[pair * PAIR * P : (pair + 1) * PAIR * P, :]
+                if pair < PAIRS - 1:
+                    nc.gpsimd.tensor_tensor(total[:], weighted[0][:], weighted[1][:], ALU.add)
+                    nc.sync.dma_start(
+                        rows.rearrange("(k p) j -> p k j", p=P), total[:].rearrange("p (k j) -> p k j", j=PICKED)
+                    )
+                else:
+                    for k in range(PAIR):
+                        cols = slice(k * PICKED, (k + 1) * PICKED)
+                        nc.vector.tensor_tensor(total[:, cols], weighted[0][:, cols], weighted[1][:, cols], ALU.add)
+                        nc.sync.dma_start(rows[k * P : (k + 1) * P, :], total[:, cols])

@@ -84,7 +84,10 @@ def tile_multiheadefralayer_nomp_kernel(tc, table, wq, wk, offs, out):
                 for h in range(HEADS):
                     key_ps = proj_psum.tile([P, PROJ_COLS], F32, tag="proj")
                     nc.tensor.matmul(key_ps[:], wk_sb[:, h * P : (h + 1) * P], table_sb[:, cols], start=True, stop=True)
-                    nc.vector.tensor_copy(key_bf[h][:, cols], key_ps[:])
+                    if c == 0:
+                        nc.scalar.copy(key_bf[h][:, cols], key_ps[:])
+                    else:
+                        nc.vector.tensor_copy(key_bf[h][:, cols], key_ps[:])
                 for b in range(c * BLOCKS_PER_PROJ, (c + 1) * BLOCKS_PER_PROJ):
                     for h, (flat, steep) in enumerate(terms):
                         x = raw_scores(exp_psum, h, b)

@@ -120,31 +120,29 @@ def tile_multiheadefralayer_nomp_kernel(tc, table, wq, wk, offs, out):
 
         with (
             tc.psum_pool(name="out_psum", bufs=8) as out_psum,
-            tc.tile_pool(name="out_work", bufs=3) as out_work,
+            tc.tile_pool(name="out_work", bufs=4) as out_work,
         ):
-            for pair in range(PAIRS):
+            first_blocks = list(range(0, BLOCKS - PAIR, PAIR)) + list(range(BLOCKS - PAIR, BLOCKS))
+            for b0, b1 in zip(first_blocks, first_blocks[1:] + [BLOCKS]):
+                width = (b1 - b0) * PICKED
                 weighted = []
                 for h in range(HEADS):
                     a = out_work.tile([P, PAIR * PICKED], F32, name="a")
-                    pair_cols = slice(pair * PAIR * PICKED, (pair + 1) * PAIR * PICKED)
-                    nc.scalar.activation(a[:], kept[h][:, pair_cols], FUNC.Sigmoid, bias=sig_bias[h], scale=-1.0)
+                    nc.scalar.activation(
+                        a[:, :width], kept[h][:, b0 * PICKED : b1 * PICKED], FUNC.Sigmoid, bias=sig_bias[h], scale=-1.0
+                    )
                     half_as = out_work.tile([P, PAIR * PICKED], F32, name=f"half_as{h}")
-                    for k in range(PAIR):
-                        cols = slice(k * PICKED, (k + 1) * PICKED)
-                        x = raw_scores(out_psum, h, pair * PAIR + k)
+                    for b in range(b0, b1):
+                        cols = slice((b - b0) * PICKED, (b - b0 + 1) * PICKED)
+                        x = raw_scores(out_psum, h, b)
                         nc.vector.scalar_tensor_tensor(
                             half_as[:, cols], x[:], 0.5 * INV_SQRT_DK, a[:, cols], ALU.mult, ALU.mult
                         )
                     weighted.append(half_as)
+                adder = nc.gpsimd if b1 - b0 == PAIR else nc.vector
                 total = out_work.tile([P, PAIR * PICKED], F32, name="total")
-                rows = out[pair * PAIR * P : (pair + 1) * PAIR * P, :]
-                if pair < PAIRS - 1:
-                    nc.gpsimd.tensor_tensor(total[:], weighted[0][:], weighted[1][:], ALU.add)
-                    nc.sync.dma_start(
-                        rows.rearrange("(k p) j -> p k j", p=P), total[:].rearrange("p (k j) -> p k j", j=PICKED)
-                    )
-                else:
-                    for k in range(PAIR):
-                        cols = slice(k * PICKED, (k + 1) * PICKED)
-                        nc.vector.tensor_tensor(total[:, cols], weighted[0][:, cols], weighted[1][:, cols], ALU.add)
-                        nc.sync.dma_start(rows[k * P : (k + 1) * P, :], total[:, cols])
+                adder.tensor_tensor(total[:, :width], weighted[0][:, :width], weighted[1][:, :width], ALU.add)
+                nc.sync.dma_start(
+                    out[b0 * P : b1 * P, :].rearrange("(k p) j -> p k j", p=P),
+                    total[:, :width].rearrange("p (k j) -> p k j", j=PICKED),
+                )

@@ -73,21 +73,23 @@ def tile_multiheadefralayer_nomp_kernel(tc, table, wq, wk, offs, out):
             tc.psum_pool(name="exp_psum", bufs=6) as exp_psum,
             tc.tile_pool(name="exp_work", bufs=4) as exp_work,
         ):
-            for h in range(HEADS):
-                q_ps = proj_psum.tile([P, PICKED], F32, tag="proj")
-                nc.tensor.matmul(
-                    q_ps[:], wq_sb[:, h * P : (h + 1) * P], table_sb[:].indirect(offsets[:]), start=True, stop=True
-                )
-                nc.vector.tensor_copy(q_bf[h][:], q_ps[:])
             for c in range(GENES // PROJ_COLS):
                 cols = slice(c * PROJ_COLS, (c + 1) * PROJ_COLS)
                 for h in range(HEADS):
                     key_ps = proj_psum.tile([P, PROJ_COLS], F32, tag="proj")
                     nc.tensor.matmul(key_ps[:], wk_sb[:, h * P : (h + 1) * P], table_sb[:, cols], start=True, stop=True)
-                    if c == 0:
-                        nc.scalar.copy(key_bf[h][:, cols], key_ps[:])
-                    else:
-                        nc.vector.tensor_copy(key_bf[h][:, cols], key_ps[:])
+                    nc.vector.tensor_copy(key_bf[h][:, cols], key_ps[:])
+                if c == 0:
+                    for h in range(HEADS):
+                        q_ps = proj_psum.tile([P, PICKED], F32, tag="proj")
+                        nc.tensor.matmul(
+                            q_ps[:],
+                            wq_sb[:, h * P : (h + 1) * P],
+                            table_sb[:].indirect(offsets[:]),
+                            start=True,
+                            stop=True,
+                        )
+                        nc.vector.tensor_copy(q_bf[h][:], q_ps[:])
                 for b in range(c * BLOCKS_PER_PROJ, (c + 1) * BLOCKS_PER_PROJ):
                     for h, (flat, steep) in enumerate(terms):
                         x = raw_scores(exp_psum, h, b)
@@ -120,29 +122,31 @@ def tile_multiheadefralayer_nomp_kernel(tc, table, wq, wk, offs, out):
 
         with (
             tc.psum_pool(name="out_psum", bufs=8) as out_psum,
-            tc.tile_pool(name="out_work", bufs=4) as out_work,
+            tc.tile_pool(name="out_work", bufs=3) as out_work,
         ):
-            first_blocks = list(range(0, BLOCKS - PAIR, PAIR)) + list(range(BLOCKS - PAIR, BLOCKS))
-            for b0, b1 in zip(first_blocks, first_blocks[1:] + [BLOCKS]):
-                width = (b1 - b0) * PICKED
+            for pair in range(PAIRS):
                 weighted = []
                 for h in range(HEADS):
                     a = out_work.tile([P, PAIR * PICKED], F32, name="a")
-                    nc.scalar.activation(
-                        a[:, :width], kept[h][:, b0 * PICKED : b1 * PICKED], FUNC.Sigmoid, bias=sig_bias[h], scale=-1.0
-                    )
+                    pair_cols = slice(pair * PAIR * PICKED, (pair + 1) * PAIR * PICKED)
+                    nc.scalar.activation(a[:], kept[h][:, pair_cols], FUNC.Sigmoid, bias=sig_bias[h], scale=-1.0)
                     half_as = out_work.tile([P, PAIR * PICKED], F32, name=f"half_as{h}")
-                    for b in range(b0, b1):
-                        cols = slice((b - b0) * PICKED, (b - b0 + 1) * PICKED)
-                        x = raw_scores(out_psum, h, b)
+                    for k in range(PAIR):
+                        cols = slice(k * PICKED, (k + 1) * PICKED)
+                        x = raw_scores(out_psum, h, pair * PAIR + k)
                         nc.vector.scalar_tensor_tensor(
                             half_as[:, cols], x[:], 0.5 * INV_SQRT_DK, a[:, cols], ALU.mult, ALU.mult
                         )
                     weighted.append(half_as)
-                adder = nc.gpsimd if b1 - b0 == PAIR else nc.vector
                 total = out_work.tile([P, PAIR * PICKED], F32, name="total")
-                adder.tensor_tensor(total[:, :width], weighted[0][:, :width], weighted[1][:, :width], ALU.add)
-                nc.sync.dma_start(
-                    out[b0 * P : b1 * P, :].rearrange("(k p) j -> p k j", p=P),
-                    total[:, :width].rearrange("p (k j) -> p k j", j=PICKED),
-                )
+                rows = out[pair * PAIR * P : (pair + 1) * PAIR * P, :]
+                if pair < PAIRS - 1:
+                    nc.gpsimd.tensor_tensor(total[:], weighted[0][:], weighted[1][:], ALU.add)
+                    nc.sync.dma_start(
+                        rows.rearrange("(k p) j -> p k j", p=P), total[:].rearrange("p (k j) -> p k j", j=PICKED)
+                    )
+                else:
+                    for k in range(PAIR):
+                        cols = slice(k * PICKED, (k + 1) * PICKED)
+                        nc.vector.tensor_tensor(total[:, cols], weighted[0][:, cols], weighted[1][:, cols], ALU.add)
+                        nc.sync.dma_start(rows[k * P : (k + 1) * P, :], total[:, cols])

@@ -15,28 +15,26 @@ PICKED = 512
 BLOCKS = GENES // P
 LOAD_COLS = 1024
 PROJ_COLS = 512
-BLOCKS_PER_PROJ = PROJ_COLS // P
 PAIR = 2
 PAIRS = BLOCKS // PAIR
+PAIR_COLS = PAIR * PICKED
+PAIRS_PER_PROJ = PROJ_COLS // (PAIR * P)
 
 EV_A = ((1.0, 0.3, -0.2), (0.8, -0.3, 0.25))
 EV_B = ((0.2, -0.3, 0.1), (-0.15, 0.25, 0.3))
 INV_SQRT_DK = 1.0 / math.sqrt(P)
-LN_TOP = 2.0**63
+
+F0, G0 = [(EV_A[0][e] - EV_A[0][0], EV_B[0][e] - EV_B[0][0]) for e in (1, 2)]
+G1, F1 = [(EV_A[1][e] - EV_A[1][0], EV_B[1][e] - EV_B[1][0]) for e in (1, 2)]
+assert abs(G1[0] - 2.0 * F1[0]) < 1e-12
+T1 = (G1[0] / 2.0, G1[1] / 2.0)
+ALPHA = math.exp(F1[1] - T1[1])
 
 FLOPS = 2 * P * HEADS * P * (PICKED + GENES) + 2 * HEADS * P * GENES * PICKED
 
 
-def flat_and_steep(h):
-    terms = [(EV_A[h][e] - EV_A[h][0], EV_B[h][e] - EV_B[h][0]) for e in (1, 2)]
-    flat, steep = sorted(terms, reverse=True)
-    assert steep[0] < flat[0] and steep[0] < 0.0
-    return flat, steep
-
-
 def tile_multiheadefralayer_nomp_kernel(tc, table, wq, wk, offs, out):
     nc = tc.nc
-    terms = [flat_and_steep(h) for h in range(HEADS)]
 
     with tc.tile_pool(name="held", bufs=1) as held:
         offsets = held.tile([P, PICKED // 16], U16, name="offsets")
@@ -50,75 +48,81 @@ def tile_multiheadefralayer_nomp_kernel(tc, table, wq, wk, offs, out):
             cols = slice(c * LOAD_COLS, (c + 1) * LOAD_COLS)
             nc.sync.dma_start(table_sb[:, cols], table[:, cols])
 
-        consts = held.tile([P, 1 + 2 * HEADS], F32, name="consts")
-        one = consts[:, 0:1]
+        consts = held.tile([P, 4], F32, name="consts")
+        bias_f0, bias_g0, bias_t1, one = [consts[:, n : n + 1] for n in range(4)]
+        nc.vector.memset(bias_f0, F0[1])
+        nc.vector.memset(bias_g0, G0[1])
+        nc.vector.memset(bias_t1, T1[1])
         nc.vector.memset(one, 1.0)
-        exp_bias = [consts[:, 1 + h : 2 + h] for h in range(HEADS)]
-        sig_bias = [consts[:, 1 + HEADS + h : 2 + HEADS + h] for h in range(HEADS)]
-        for h, (flat, steep) in enumerate(terms):
-            nc.vector.memset(exp_bias[h], steep[1] - flat[1])
-            nc.vector.memset(sig_bias[h], -flat[1])
 
         q_bf = [held.tile([P, PICKED], BF16, name=f"q_bf{h}") for h in range(HEADS)]
         key_bf = [held.tile([P, GENES], BF16, name=f"key_bf{h}") for h in range(HEADS)]
-        kept = [held.tile([P, BLOCKS * PICKED], F32, name=f"kept{h}") for h in range(HEADS)]
+        d0_squared = held.tile([P, BLOCKS * PICKED], F32, name="d0_squared")
+        d1_squared_less_1 = held.tile([P, BLOCKS * PICKED], F32, name="d1_squared_less_1")
 
         def raw_scores(psum, h, b):
             x = psum.tile([P, PICKED], F32, name="x")
             nc.tensor.matmul(x[:], key_bf[h][:, b * P : (b + 1) * P], q_bf[h][:], start=True, stop=True)
             return x
 
+        def pair_cols(pair):
+            return slice(pair * PAIR_COLS, (pair + 1) * PAIR_COLS)
+
         with (
             tc.psum_pool(name="proj_psum", bufs=2) as proj_psum,
             tc.psum_pool(name="exp_psum", bufs=6) as exp_psum,
-            tc.tile_pool(name="exp_work", bufs=4) as exp_work,
+            tc.tile_pool(name="exp_work", bufs=3) as exp_work,
         ):
-            for c in range(GENES // PROJ_COLS):
+            for_scalar = []
+
+            def project_keys(c):
                 cols = slice(c * PROJ_COLS, (c + 1) * PROJ_COLS)
                 for h in range(HEADS):
-                    key_ps = proj_psum.tile([P, PROJ_COLS], F32, tag="proj")
-                    nc.tensor.matmul(key_ps[:], wk_sb[:, h * P : (h + 1) * P], table_sb[:, cols], start=True, stop=True)
+                    key_ps = proj_psum.tile([P, PROJ_COLS], BF16, tag="proj")
+                    nc.tensor.matmul(
+                        key_ps[:], wk_sb[:, h * P : (h + 1) * P], table_sb[:, cols], start=True, stop=True
+                    )
                     nc.vector.tensor_copy(key_bf[h][:, cols], key_ps[:])
-                if c == 0:
-                    for h in range(HEADS):
-                        q_ps = proj_psum.tile([P, PICKED], F32, tag="proj")
-                        nc.tensor.matmul(
-                            q_ps[:],
-                            wq_sb[:, h * P : (h + 1) * P],
-                            table_sb[:].indirect(offsets[:]),
-                            start=True,
-                            stop=True,
-                        )
-                        nc.vector.tensor_copy(q_bf[h][:], q_ps[:])
-                for b in range(c * BLOCKS_PER_PROJ, (c + 1) * BLOCKS_PER_PROJ):
-                    for h, (flat, steep) in enumerate(terms):
-                        x = raw_scores(exp_psum, h, b)
-                        r = exp_work.tile([P, PICKED], F32, name="r")
-                        nc.scalar.activation(
-                            r[:], x[:], FUNC.Exp, bias=exp_bias[h], scale=(steep[0] - flat[0]) * INV_SQRT_DK
-                        )
-                        nc.vector.tensor_scalar_min(kept[h][:, b * PICKED : (b + 1) * PICKED], r[:], LN_TOP)
 
-        with (
-            tc.psum_pool(name="log_psum", bufs=8) as log_psum,
-            tc.tile_pool(name="log_work", bufs=4) as log_work,
-        ):
+            project_keys(0)
+            for h in range(HEADS):
+                q_ps = proj_psum.tile([P, PICKED], F32, tag="proj")
+                nc.tensor.matmul(
+                    q_ps[:], wq_sb[:, h * P : (h + 1) * P], table_sb[:].indirect(offsets[:]), start=True, stop=True
+                )
+                nc.vector.tensor_copy(q_bf[h][:], q_ps[:])
+
             for pair in range(PAIRS):
-                for h, (flat, steep) in enumerate(terms):
-                    log1p = log_work.tile([P, PAIR * PICKED], F32, name="log1p")
-                    pair_cols = slice(pair * PAIR * PICKED, (pair + 1) * PAIR * PICKED)
-                    nc.scalar.activation(log1p[:], kept[h][:, pair_cols], FUNC.Ln, bias=one, scale=1.0)
-                    for k in range(PAIR):
-                        b = pair * PAIR + k
-                        x = raw_scores(log_psum, h, b)
-                        nc.vector.scalar_tensor_tensor(
-                            kept[h][:, b * PICKED : (b + 1) * PICKED],
-                            x[:],
-                            flat[0] * INV_SQRT_DK,
-                            log1p[:, k * PICKED : (k + 1) * PICKED],
-                            ALU.mult,
-                            ALU.add,
-                        )
+                if pair % PAIRS_PER_PROJ == 0 and pair // PAIRS_PER_PROJ + 1 < GENES // PROJ_COLS:
+                    project_keys(pair // PAIRS_PER_PROJ + 1)
+
+                exp_f0 = exp_work.tile([P, PAIR_COLS], F32, name="exp_f0")
+                exp_g0 = exp_work.tile([P, PAIR_COLS], F32, name="exp_g0")
+                t1 = exp_work.tile([P, PAIR_COLS], F32, name="t1")
+                for k in range(PAIR):
+                    cols = slice(k * PICKED, (k + 1) * PICKED)
+                    x0 = raw_scores(exp_psum, 0, pair * PAIR + k)
+                    nc.scalar.activation(exp_f0[:, cols], x0[:], FUNC.Exp, bias=bias_f0, scale=F0[0] * INV_SQRT_DK)
+                    nc.scalar.activation(exp_g0[:, cols], x0[:], FUNC.Exp, bias=bias_g0, scale=G0[0] * INV_SQRT_DK)
+                    x1 = raw_scores(exp_psum, 1, pair * PAIR + k)
+                    nc.scalar.activation(t1[:, cols], x1[:], FUNC.Exp, bias=bias_t1, scale=T1[0] * INV_SQRT_DK)
+                for earlier_pair, earlier_d0 in for_scalar:
+                    nc.scalar.activation(d0_squared[:, pair_cols(earlier_pair)], earlier_d0[:], FUNC.Square)
+                for_scalar.clear()
+
+                d0 = exp_work.tile([P, PAIR_COLS], F32, name="d0")
+                nc.vector.scalar_tensor_tensor(d0[:], exp_f0[:], 1.0, exp_g0[:], ALU.add, ALU.add)
+                if pair % 2 == 0:
+                    nc.vector.tensor_tensor(d0_squared[:, pair_cols(pair)], d0[:], d0[:], ALU.mult)
+                else:
+                    for_scalar.append((pair, d0))
+                d1_less_1 = exp_work.tile([P, PAIR_COLS], F32, name="d1_less_1")
+                nc.vector.scalar_tensor_tensor(d1_less_1[:], t1[:], ALPHA, t1[:], ALU.add, ALU.mult)
+                nc.vector.scalar_tensor_tensor(
+                    d1_squared_less_1[:, pair_cols(pair)], d1_less_1[:], 2.0, d1_less_1[:], ALU.add, ALU.mult
+                )
+            for earlier_pair, earlier_d0 in for_scalar:
+                nc.scalar.activation(d0_squared[:, pair_cols(earlier_pair)], earlier_d0[:], FUNC.Square)
 
         with (
             tc.psum_pool(name="out_psum", bufs=8) as out_psum,
@@ -127,10 +131,14 @@ def tile_multiheadefralayer_nomp_kernel(tc, table, wq, wk, offs, out):
             for pair in range(PAIRS):
                 weighted = []
                 for h in range(HEADS):
-                    a = out_work.tile([P, PAIR * PICKED], F32, name="a")
-                    pair_cols = slice(pair * PAIR * PICKED, (pair + 1) * PAIR * PICKED)
-                    nc.scalar.activation(a[:], kept[h][:, pair_cols], FUNC.Sigmoid, bias=sig_bias[h], scale=-1.0)
-                    half_as = out_work.tile([P, PAIR * PICKED], F32, name=f"half_as{h}")
+                    a = out_work.tile([P, PAIR_COLS], F32, name="a")
+                    if h == 0:
+                        nc.scalar.activation(a[:], d0_squared[:, pair_cols(pair)], FUNC.Abs_reciprocal_sqrt)
+                    else:
+                        nc.scalar.activation(
+                            a[:], d1_squared_less_1[:, pair_cols(pair)], FUNC.Abs_reciprocal_sqrt, bias=one
+                        )
+                    half_as = out_work.tile([P, PAIR_COLS], F32, name=f"half_as{h}")
                     for k in range(PAIR):
                         cols = slice(k * PICKED, (k + 1) * PICKED)
                         x = raw_scores(out_psum, h, pair * PAIR + k)
@@ -138,7 +146,7 @@ def tile_multiheadefralayer_nomp_kernel(tc, table, wq, wk, offs, out):
                             half_as[:, cols], x[:], 0.5 * INV_SQRT_DK, a[:, cols], ALU.mult, ALU.mult
                         )
                     weighted.append(half_as)
-                total = out_work.tile([P, PAIR * PICKED], F32, name="total")
+                total = out_work.tile([P, PAIR_COLS], F32, name="total")
                 rows = out[pair * PAIR * P : (pair + 1) * PAIR * P, :]
                 if pair < PAIRS - 1:
                     nc.gpsimd.tensor_tensor(total[:], weighted[0][:], weighted[1][:], ALU.add)

@@ -70,10 +70,13 @@ def tile_multiheadefralayer_nomp_kernel(tc, table, wq, wk, offs, out):
 
         with (
             tc.psum_pool(name="proj_psum", bufs=2) as proj_psum,
-            tc.psum_pool(name="exp_psum", bufs=6) as exp_psum,
-            tc.tile_pool(name="exp_work", bufs=3) as exp_work,
+            tc.psum_pool(name="score_psum", bufs=6) as score_psum,
+            tc.tile_pool(name="work", bufs=3) as work,
         ):
-            for_scalar = []
+
+            def work_tile(name, ring):
+                return work.tile([P, PAIR_COLS], F32, name=name, tag=f"ring{ring}")
+
 
             def project_keys(c):
                 cols = slice(c * PROJ_COLS, (c + 1) * PROJ_COLS)
@@ -96,57 +99,49 @@ def tile_multiheadefralayer_nomp_kernel(tc, table, wq, wk, offs, out):
                 if pair % PAIRS_PER_PROJ == 0 and pair // PAIRS_PER_PROJ + 1 < GENES // PROJ_COLS:
                     project_keys(pair // PAIRS_PER_PROJ + 1)
 
-                exp_f0 = exp_work.tile([P, PAIR_COLS], F32, name="exp_f0")
-                exp_g0 = exp_work.tile([P, PAIR_COLS], F32, name="exp_g0")
-                t1 = exp_work.tile([P, PAIR_COLS], F32, name="t1")
+                exp_f0 = work_tile("exp_f0", 0)
+                exp_g0 = work_tile("exp_g0", 1)
+                t1 = work_tile("t1", 2)
                 for k in range(PAIR):
                     cols = slice(k * PICKED, (k + 1) * PICKED)
-                    x0 = raw_scores(exp_psum, 0, pair * PAIR + k)
+                    x0 = raw_scores(score_psum, 0, pair * PAIR + k)
                     nc.scalar.activation(exp_f0[:, cols], x0[:], FUNC.Exp, bias=bias_f0, scale=F0[0] * INV_SQRT_DK)
                     nc.scalar.activation(exp_g0[:, cols], x0[:], FUNC.Exp, bias=bias_g0, scale=G0[0] * INV_SQRT_DK)
-                    x1 = raw_scores(exp_psum, 1, pair * PAIR + k)
+                    x1 = raw_scores(score_psum, 1, pair * PAIR + k)
                     nc.scalar.activation(t1[:, cols], x1[:], FUNC.Exp, bias=bias_t1, scale=T1[0] * INV_SQRT_DK)
-                for earlier_pair, earlier_d0 in for_scalar:
-                    nc.scalar.activation(d0_squared[:, pair_cols(earlier_pair)], earlier_d0[:], FUNC.Square)
-                for_scalar.clear()
 
-                d0 = exp_work.tile([P, PAIR_COLS], F32, name="d0")
+                d0 = work_tile("d0", 3)
                 nc.vector.scalar_tensor_tensor(d0[:], exp_f0[:], 1.0, exp_g0[:], ALU.add, ALU.add)
-                if pair % 2 == 0:
-                    nc.vector.tensor_tensor(d0_squared[:, pair_cols(pair)], d0[:], d0[:], ALU.mult)
-                else:
-                    for_scalar.append((pair, d0))
-                d1_less_1 = exp_work.tile([P, PAIR_COLS], F32, name="d1_less_1")
+                first = pair * PAIR_COLS
+                nc.vector.tensor_tensor(
+                    d0_squared[:, first : first + PICKED], d0[:, :PICKED], d0[:, :PICKED], ALU.mult
+                )
+                nc.scalar.activation(d0_squared[:, first + PICKED : first + PAIR_COLS], d0[:, PICKED:], FUNC.Square)
+                d1_less_1 = work_tile("d1_less_1", 4)
                 nc.vector.scalar_tensor_tensor(d1_less_1[:], t1[:], ALPHA, t1[:], ALU.add, ALU.mult)
                 nc.vector.scalar_tensor_tensor(
                     d1_squared_less_1[:, pair_cols(pair)], d1_less_1[:], 2.0, d1_less_1[:], ALU.add, ALU.mult
                 )
-            for earlier_pair, earlier_d0 in for_scalar:
-                nc.scalar.activation(d0_squared[:, pair_cols(earlier_pair)], earlier_d0[:], FUNC.Square)
 
-        with (
-            tc.psum_pool(name="out_psum", bufs=8) as out_psum,
-            tc.tile_pool(name="out_work", bufs=3) as out_work,
-        ):
             for pair in range(PAIRS):
                 weighted = []
                 for h in range(HEADS):
-                    a = out_work.tile([P, PAIR_COLS], F32, name="a")
+                    a = work_tile("a", 0)
                     if h == 0:
                         nc.scalar.activation(a[:], d0_squared[:, pair_cols(pair)], FUNC.Abs_reciprocal_sqrt)
                     else:
                         nc.scalar.activation(
                             a[:], d1_squared_less_1[:, pair_cols(pair)], FUNC.Abs_reciprocal_sqrt, bias=one
                         )
-                    half_as = out_work.tile([P, PAIR_COLS], F32, name=f"half_as{h}")
+                    half_as = work_tile(f"half_as{h}", 1 + h)
                     for k in range(PAIR):
                         cols = slice(k * PICKED, (k + 1) * PICKED)
-                        x = raw_scores(out_psum, h, pair * PAIR + k)
+                        x = raw_scores(score_psum, h, pair * PAIR + k)
                         nc.vector.scalar_tensor_tensor(
                             half_as[:, cols], x[:], 0.5 * INV_SQRT_DK, a[:, cols], ALU.mult, ALU.mult
                         )
                     weighted.append(half_as)
-                total = out_work.tile([P, PAIR_COLS], F32, name="total")
+                total = work_tile("total", 3)
                 rows = out[pair * PAIR * P : (pair + 1) * PAIR * P, :]
                 if pair < PAIRS - 1:
                     nc.gpsimd.tensor_tensor(total[:], weighted[0][:], weighted[1][:], ALU.add)

@@ -10,6 +10,7 @@ ALU = mybir.AluOpType
 
 P = 128
 HEADS = 2
+HEAD_1_FIRST = (1, 0)
 GENES = 4096
 PICKED = 512
 BLOCKS = GENES // P
@@ -18,7 +19,6 @@ PROJ_COLS = 512
 PAIR = 2
 PAIRS = BLOCKS // PAIR
 PAIR_COLS = PAIR * PICKED
-PAIRS_PER_PROJ = PROJ_COLS // (PAIR * P)
 
 EV_A = ((1.0, 0.3, -0.2), (0.8, -0.3, 0.25))
 EV_B = ((0.2, -0.3, 0.1), (-0.15, 0.25, 0.3))
@@ -71,7 +71,7 @@ def tile_multiheadefralayer_nomp_kernel(tc, table, wq, wk, offs, out):
         with (
             tc.psum_pool(name="proj_psum", bufs=2) as proj_psum,
             tc.psum_pool(name="score_psum", bufs=6) as score_psum,
-            tc.tile_pool(name="work", bufs=3) as work,
+            tc.tile_pool(name="work", bufs=4) as work,
         ):
 
             def work_tile(name, ring):
@@ -88,28 +88,36 @@ def tile_multiheadefralayer_nomp_kernel(tc, table, wq, wk, offs, out):
                     nc.vector.tensor_copy(key_bf[h][:, cols], key_ps[:])
 
             project_keys(0)
-            for h in range(HEADS):
+            for h in HEAD_1_FIRST:
                 q_ps = proj_psum.tile([P, PICKED], F32, tag="proj")
                 nc.tensor.matmul(
                     q_ps[:], wq_sb[:, h * P : (h + 1) * P], table_sb[:].indirect(offsets[:]), start=True, stop=True
                 )
                 nc.vector.tensor_copy(q_bf[h][:], q_ps[:])
 
+            for c in range(1, GENES // PROJ_COLS):
+                project_keys(c)
+
             for pair in range(PAIRS):
-                if pair % PAIRS_PER_PROJ == 0 and pair // PAIRS_PER_PROJ + 1 < GENES // PROJ_COLS:
-                    project_keys(pair // PAIRS_PER_PROJ + 1)
+                t1 = work_tile("t1", 2)
+                for k in range(PAIR):
+                    x1 = raw_scores(score_psum, 1, pair * PAIR + k)
+                    nc.scalar.activation(
+                        t1[:, k * PICKED : (k + 1) * PICKED], x1[:], FUNC.Exp, bias=bias_t1, scale=T1[0] * INV_SQRT_DK
+                    )
+                d1_less_1 = work_tile("d1_less_1", 4)
+                nc.vector.scalar_tensor_tensor(d1_less_1[:], t1[:], ALPHA, t1[:], ALU.add, ALU.mult)
+                nc.vector.scalar_tensor_tensor(
+                    d1_squared_less_1[:, pair_cols(pair)], d1_less_1[:], 2.0, d1_less_1[:], ALU.add, ALU.mult
+                )
 
                 exp_f0 = work_tile("exp_f0", 0)
                 exp_g0 = work_tile("exp_g0", 1)
-                t1 = work_tile("t1", 2)
                 for k in range(PAIR):
                     cols = slice(k * PICKED, (k + 1) * PICKED)
                     x0 = raw_scores(score_psum, 0, pair * PAIR + k)
                     nc.scalar.activation(exp_f0[:, cols], x0[:], FUNC.Exp, bias=bias_f0, scale=F0[0] * INV_SQRT_DK)
                     nc.scalar.activation(exp_g0[:, cols], x0[:], FUNC.Exp, bias=bias_g0, scale=G0[0] * INV_SQRT_DK)
-                    x1 = raw_scores(score_psum, 1, pair * PAIR + k)
-                    nc.scalar.activation(t1[:, cols], x1[:], FUNC.Exp, bias=bias_t1, scale=T1[0] * INV_SQRT_DK)
-
                 d0 = work_tile("d0", 3)
                 nc.vector.scalar_tensor_tensor(d0[:], exp_f0[:], 1.0, exp_g0[:], ALU.add, ALU.add)
                 first = pair * PAIR_COLS
@@ -117,11 +125,6 @@ def tile_multiheadefralayer_nomp_kernel(tc, table, wq, wk, offs, out):
                     d0_squared[:, first : first + PICKED], d0[:, :PICKED], d0[:, :PICKED], ALU.mult
                 )
                 nc.scalar.activation(d0_squared[:, first + PICKED : first + PAIR_COLS], d0[:, PICKED:], FUNC.Square)
-                d1_less_1 = work_tile("d1_less_1", 4)
-                nc.vector.scalar_tensor_tensor(d1_less_1[:], t1[:], ALPHA, t1[:], ALU.add, ALU.mult)
-                nc.vector.scalar_tensor_tensor(
-                    d1_squared_less_1[:, pair_cols(pair)], d1_less_1[:], 2.0, d1_less_1[:], ALU.add, ALU.mult
-                )
 
             for pair in range(PAIRS):
                 weighted = []

@@ -19,6 +19,7 @@ PROJ_COLS = 512
 PAIR = 2
 PAIRS = BLOCKS // PAIR
 PAIR_COLS = PAIR * PICKED
+PAIRS_SUMMED_BY_VECTOR = 2
 
 EV_A = ((1.0, 0.3, -0.2), (0.8, -0.3, 0.25))
 EV_B = ((0.2, -0.3, 0.1), (-0.15, 0.25, 0.3))
@@ -126,6 +127,7 @@ def tile_multiheadefralayer_nomp_kernel(tc, table, wq, wk, offs, out):
                 )
                 nc.scalar.activation(d0_squared[:, first + PICKED : first + PAIR_COLS], d0[:, PICKED:], FUNC.Square)
 
+            left_to_vector = []
             for pair in range(PAIRS):
                 weighted = []
                 for h in range(HEADS):
@@ -144,15 +146,20 @@ def tile_multiheadefralayer_nomp_kernel(tc, table, wq, wk, offs, out):
                             half_as[:, cols], x[:], 0.5 * INV_SQRT_DK, a[:, cols], ALU.mult, ALU.mult
                         )
                     weighted.append(half_as)
-                total = work_tile("total", 3)
-                rows = out[pair * PAIR * P : (pair + 1) * PAIR * P, :]
-                if pair < PAIRS - 1:
+                if pair < PAIRS - PAIRS_SUMMED_BY_VECTOR:
+                    total = work_tile("total", 3)
                     nc.gpsimd.tensor_tensor(total[:], weighted[0][:], weighted[1][:], ALU.add)
                     nc.sync.dma_start(
-                        rows.rearrange("(k p) j -> p k j", p=P), total[:].rearrange("p (k j) -> p k j", j=PICKED)
+                        out[pair * PAIR * P : (pair + 1) * PAIR * P, :].rearrange("(k p) j -> p k j", p=P),
+                        total[:].rearrange("p (k j) -> p k j", j=PICKED),
                     )
                 else:
-                    for k in range(PAIR):
-                        cols = slice(k * PICKED, (k + 1) * PICKED)
-                        nc.vector.tensor_tensor(total[:, cols], weighted[0][:, cols], weighted[1][:, cols], ALU.add)
-                        nc.sync.dma_start(rows[k * P : (k + 1) * P, :], total[:, cols])
+                    left_to_vector.append((pair, weighted))
+
+            for pair, weighted in left_to_vector:
+                total = work_tile("total", 3)
+                for k in range(PAIR):
+                    cols = slice(k * PICKED, (k + 1) * PICKED)
+                    b = pair * PAIR + k
+                    nc.vector.tensor_tensor(total[:, cols], weighted[0][:, cols], weighted[1][:, cols], ALU.add)
+                    nc.sync.dma_start(out[b * P : (b + 1) * P, :], total[:, cols])

@@ -94,7 +94,7 @@ def tile_multiheadefralayer_nomp_kernel(tc, table, wq, wk, offs, out):
                 nc.tensor.matmul(
                     q_ps[:], wq_sb[:, h * P : (h + 1) * P], table_sb[:].indirect(offsets[:]), start=True, stop=True
                 )
-                nc.vector.tensor_copy(q_bf[h][:], q_ps[:])
+                nc.scalar.copy(q_bf[h][:], q_ps[:])
 
             for c in range(1, GENES // PROJ_COLS):
                 project_keys(c)

@@ -49,13 +49,6 @@ def tile_multiheadefralayer_nomp_kernel(tc, table, wq, wk, offs, out):
             cols = slice(c * LOAD_COLS, (c + 1) * LOAD_COLS)
             nc.sync.dma_start(table_sb[:, cols], table[:, cols])
 
-        consts = held.tile([P, 4], F32, name="consts")
-        bias_f0, bias_g0, bias_t1, one = [consts[:, n : n + 1] for n in range(4)]
-        nc.vector.memset(bias_f0, F0[1])
-        nc.vector.memset(bias_g0, G0[1])
-        nc.vector.memset(bias_t1, T1[1])
-        nc.vector.memset(one, 1.0)
-
         q_bf = [held.tile([P, PICKED], BF16, name=f"q_bf{h}") for h in range(HEADS)]
         key_bf = [held.tile([P, GENES], BF16, name=f"key_bf{h}") for h in range(HEADS)]
         d0_squared = held.tile([P, BLOCKS * PICKED], F32, name="d0_squared")
@@ -104,7 +97,7 @@ def tile_multiheadefralayer_nomp_kernel(tc, table, wq, wk, offs, out):
                 for k in range(PAIR):
                     x1 = raw_scores(score_psum, 1, pair * PAIR + k)
                     nc.scalar.activation(
-                        t1[:, k * PICKED : (k + 1) * PICKED], x1[:], FUNC.Exp, bias=bias_t1, scale=T1[0] * INV_SQRT_DK
+                        t1[:, k * PICKED : (k + 1) * PICKED], x1[:], FUNC.Exp, bias=T1[1], scale=T1[0] * INV_SQRT_DK
                     )
                 d1_less_1 = work_tile("d1_less_1", 4)
                 nc.vector.scalar_tensor_tensor(d1_less_1[:], t1[:], ALPHA, t1[:], ALU.add, ALU.mult)
@@ -117,8 +110,8 @@ def tile_multiheadefralayer_nomp_kernel(tc, table, wq, wk, offs, out):
                 for k in range(PAIR):
                     cols = slice(k * PICKED, (k + 1) * PICKED)
                     x0 = raw_scores(score_psum, 0, pair * PAIR + k)
-                    nc.scalar.activation(exp_f0[:, cols], x0[:], FUNC.Exp, bias=bias_f0, scale=F0[0] * INV_SQRT_DK)
-                    nc.scalar.activation(exp_g0[:, cols], x0[:], FUNC.Exp, bias=bias_g0, scale=G0[0] * INV_SQRT_DK)
+                    nc.scalar.activation(exp_f0[:, cols], x0[:], FUNC.Exp, bias=F0[1], scale=F0[0] * INV_SQRT_DK)
+                    nc.scalar.activation(exp_g0[:, cols], x0[:], FUNC.Exp, bias=G0[1], scale=G0[0] * INV_SQRT_DK)
                 d0 = work_tile("d0", 3)
                 nc.vector.scalar_tensor_tensor(d0[:], exp_f0[:], 1.0, exp_g0[:], ALU.add, ALU.add)
                 first = pair * PAIR_COLS
@@ -136,7 +129,7 @@ def tile_multiheadefralayer_nomp_kernel(tc, table, wq, wk, offs, out):
                         nc.scalar.activation(a[:], d0_squared[:, pair_cols(pair)], FUNC.Abs_reciprocal_sqrt)
                     else:
                         nc.scalar.activation(
-                            a[:], d1_squared_less_1[:, pair_cols(pair)], FUNC.Abs_reciprocal_sqrt, bias=one
+                            a[:], d1_squared_less_1[:, pair_cols(pair)], FUNC.Abs_reciprocal_sqrt, bias=1.0
                         )
                     half_as = work_tile(f"half_as{h}", 1 + h)
                     for k in range(PAIR):

import math

import concourse.mybir as mybir

F32 = mybir.dt.float32
BF16 = mybir.dt.bfloat16
U16 = mybir.dt.uint16
FUNC = mybir.ActivationFunctionType
ALU = mybir.AluOpType

P = 128
HEADS = 2
HEAD_1_FIRST = (1, 0)
GENES = 4096
PICKED = 512
BLOCKS = GENES // P
LOAD_COLS = 1024
PROJ_COLS = 512
PAIR = 2
PAIRS = BLOCKS // PAIR
PAIR_COLS = PAIR * PICKED
PAIRS_SUMMED_BY_VECTOR = 2

EV_A = ((1.0, 0.3, -0.2), (0.8, -0.3, 0.25))
EV_B = ((0.2, -0.3, 0.1), (-0.15, 0.25, 0.3))
INV_SQRT_DK = 1.0 / math.sqrt(P)

F0, G0 = [(EV_A[0][e] - EV_A[0][0], EV_B[0][e] - EV_B[0][0]) for e in (1, 2)]
G1, F1 = [(EV_A[1][e] - EV_A[1][0], EV_B[1][e] - EV_B[1][0]) for e in (1, 2)]
assert abs(G1[0] - 2.0 * F1[0]) < 1e-12
T1 = (G1[0] / 2.0, G1[1] / 2.0)
ALPHA = math.exp(F1[1] - T1[1])

FLOPS = 2 * P * HEADS * P * (PICKED + GENES) + 2 * HEADS * P * GENES * PICKED


def tile_multiheadefralayer_nomp_kernel(tc, table, wq, wk, offs, out):
    nc = tc.nc

    with tc.tile_pool(name="held", bufs=1) as held:
        offsets = held.tile([P, PICKED // 16], U16, name="offsets")
        nc.sync.dma_start(offsets[:], offs)
        wq_sb = held.tile([P, HEADS * P], BF16, name="wq_sb")
        nc.scalar.dma_start(wq_sb[:], wq)
        wk_sb = held.tile([P, HEADS * P], BF16, name="wk_sb")
        nc.scalar.dma_start(wk_sb[:], wk)
        table_sb = held.tile([P, GENES], BF16, name="table_sb")
        for c in range(GENES // LOAD_COLS):
            cols = slice(c * LOAD_COLS, (c + 1) * LOAD_COLS)
            nc.sync.dma_start(table_sb[:, cols], table[:, cols])

        q_bf = [held.tile([P, PICKED], BF16, name=f"q_bf{h}") for h in range(HEADS)]
        key_bf = [held.tile([P, GENES], BF16, name=f"key_bf{h}") for h in range(HEADS)]
        d0_squared = held.tile([P, BLOCKS * PICKED], F32, name="d0_squared")
        d1_squared_less_1 = held.tile([P, BLOCKS * PICKED], F32, name="d1_squared_less_1")

        def raw_scores(psum, h, b):
            x = psum.tile([P, PICKED], F32, name="x")
            nc.tensor.matmul(x[:], key_bf[h][:, b * P : (b + 1) * P], q_bf[h][:], start=True, stop=True)
            return x

        def pair_cols(pair):
            return slice(pair * PAIR_COLS, (pair + 1) * PAIR_COLS)

        with (
            tc.psum_pool(name="proj_psum", bufs=2) as proj_psum,
            tc.psum_pool(name="score_psum", bufs=6) as score_psum,
            tc.tile_pool(name="work", bufs=4) as work,
        ):

            def work_tile(name, ring):
                return work.tile([P, PAIR_COLS], F32, name=name, tag=f"ring{ring}")


            def project_keys(c):
                cols = slice(c * PROJ_COLS, (c + 1) * PROJ_COLS)
                for h in range(HEADS):
                    key_ps = proj_psum.tile([P, PROJ_COLS], BF16, tag="proj")
                    nc.tensor.matmul(
                        key_ps[:], wk_sb[:, h * P : (h + 1) * P], table_sb[:, cols], start=True, stop=True
                    )
                    nc.vector.tensor_copy(key_bf[h][:, cols], key_ps[:])

            project_keys(0)
            for h in HEAD_1_FIRST:
                q_ps = proj_psum.tile([P, PICKED], F32, tag="proj")
                nc.tensor.matmul(
                    q_ps[:], wq_sb[:, h * P : (h + 1) * P], table_sb[:].indirect(offsets[:]), start=True, stop=True
                )
                nc.scalar.copy(q_bf[h][:], q_ps[:])

            for c in range(1, GENES // PROJ_COLS):
                project_keys(c)

            for pair in range(PAIRS):
                t1 = work_tile("t1", 2)
                for k in range(PAIR):
                    x1 = raw_scores(score_psum, 1, pair * PAIR + k)
                    nc.scalar.activation(
                        t1[:, k * PICKED : (k + 1) * PICKED], x1[:], FUNC.Exp, bias=T1[1], scale=T1[0] * INV_SQRT_DK
                    )
                d1_less_1 = work_tile("d1_less_1", 4)
                nc.vector.scalar_tensor_tensor(d1_less_1[:], t1[:], ALPHA, t1[:], ALU.add, ALU.mult)
                nc.vector.scalar_tensor_tensor(
                    d1_squared_less_1[:, pair_cols(pair)], d1_less_1[:], 2.0, d1_less_1[:], ALU.add, ALU.mult
                )

                exp_f0 = work_tile("exp_f0", 0)
                exp_g0 = work_tile("exp_g0", 1)
                for k in range(PAIR):
                    cols = slice(k * PICKED, (k + 1) * PICKED)
                    x0 = raw_scores(score_psum, 0, pair * PAIR + k)
                    nc.scalar.activation(exp_f0[:, cols], x0[:], FUNC.Exp, bias=F0[1], scale=F0[0] * INV_SQRT_DK)
                    nc.scalar.activation(exp_g0[:, cols], x0[:], FUNC.Exp, bias=G0[1], scale=G0[0] * INV_SQRT_DK)
                d0 = work_tile("d0", 3)
                nc.vector.scalar_tensor_tensor(d0[:], exp_f0[:], 1.0, exp_g0[:], ALU.add, ALU.add)
                first = pair * PAIR_COLS
                nc.vector.tensor_tensor(
                    d0_squared[:, first : first + PICKED], d0[:, :PICKED], d0[:, :PICKED], ALU.mult
                )
                nc.scalar.activation(d0_squared[:, first + PICKED : first + PAIR_COLS], d0[:, PICKED:], FUNC.Square)

            left_to_vector = []
            for pair in range(PAIRS):
                weighted = []
                for h in range(HEADS):
                    a = work_tile("a", 0)
                    if h == 0:
                        nc.scalar.activation(a[:], d0_squared[:, pair_cols(pair)], FUNC.Abs_reciprocal_sqrt)
                    else:
                        nc.scalar.activation(
                            a[:], d1_squared_less_1[:, pair_cols(pair)], FUNC.Abs_reciprocal_sqrt, bias=1.0
                        )
                    half_as = work_tile(f"half_as{h}", 1 + h)
                    for k in range(PAIR):
                        cols = slice(k * PICKED, (k + 1) * PICKED)
                        x = raw_scores(score_psum, h, pair * PAIR + k)
                        nc.vector.scalar_tensor_tensor(
                            half_as[:, cols], x[:], 0.5 * INV_SQRT_DK, a[:, cols], ALU.mult, ALU.mult
                        )
                    weighted.append(half_as)
                if pair < PAIRS - PAIRS_SUMMED_BY_VECTOR:
                    total = work_tile("total", 3)
                    nc.gpsimd.tensor_tensor(total[:], weighted[0][:], weighted[1][:], ALU.add)
                    nc.sync.dma_start(
                        out[pair * PAIR * P : (pair + 1) * PAIR * P, :].rearrange("(k p) j -> p k j", p=P),
                        total[:].rearrange("p (k j) -> p k j", j=PICKED),
                    )
                else:
                    left_to_vector.append((pair, weighted))

            for pair, weighted in left_to_vector:
                total = work_tile("total", 3)
                for k in range(PAIR):
                    cols = slice(k * PICKED, (k + 1) * PICKED)
                    b = pair * PAIR + k
                    nc.vector.tensor_tensor(total[:, cols], weighted[0][:, cols], weighted[1][:, cols], ALU.add)
                    nc.sync.dma_start(out[b * P : (b + 1) * P, :], total[:, cols])
